import numpy as np
import ml_dtypes

BF16 = ml_dtypes.bfloat16


def bf(x):
    return np.asarray(x, np.float32).astype(BF16)


def f32(x):
    return np.asarray(x, np.float32)


def f64(x):
    return np.asarray(x).astype(np.float64)


def striped(idx):
    return np.tile(idx.reshape(-1, 16).T, (8, 1))


B, T, D, H, DH, S, N = 8, 256, 512, 4, 128, 4096, 2048


def setup_inputs():
    sc = 1.0 / np.sqrt(D)
    return {
        "base": f32(0.2 * np.random.standard_normal((D, S))),
        "x_head": bf(np.random.standard_normal((D, N))),
        "x_tail": bf(np.random.standard_normal((D, N))),
        "w_head": bf(sc * np.random.standard_normal((D, D))),
        "b_head": f32(0.1 * np.random.standard_normal((D, 1))),
        "w_v": bf(sc * np.random.standard_normal((D, D))),
        "b_v": f32(0.1 * np.random.standard_normal((D, 1))),
        "w_out": bf(sc * np.random.standard_normal((D, D))),
        "b_out": f32(0.1 * np.random.standard_normal((D, 1))),
        "rel": f32(1.0 + 0.1 * np.random.standard_normal((D, 1))),
        "topo": f32(np.random.random((H, T, T)) < 0.5),
        "offs": striped(np.random.permutation(S)[:N]),
    }


def reference(base, x_head, x_tail, w_head, b_head, w_v, b_v, w_out, b_out, rel, topo, offs):
    idx = offs[:16].T.reshape(-1)
    fh = f64(w_head).T @ f64(x_head) + f64(b_head)
    ft = f64(w_head).T @ f64(x_tail) + f64(b_head)
    fv = f64(w_v).T @ f64(x_tail) + f64(b_v)
    q = (fh * f64(rel)).reshape(H, DH, B, T)
    k = ft.reshape(H, DH, B, T)
    v = fv.reshape(H, DH, B, T)
    score = np.einsum('hdbi,hdbt->bhti', q, k) / np.sqrt(DH)
    keep = f64(topo) * (1.0 - np.eye(T))[None] * (np.arange(T) > 0)[None, :, None]
    e = np.exp(score) * keep[None]
    p = e / e.sum(axis=2, keepdims=True)
    att = np.einsum('bhti,hdbt->hdbi', p, v).reshape(D, N)
    y = f64(w_out).T @ att
    out = f64(base).copy()
    out[:, idx] = y + f64(b_out)
    return out

@@ -1,0 +1,203 @@
+import math
+from itertools import product
+
+import concourse.mybir as mybir
+from concourse.masks import make_identity
+
+BF16, F32, U16 = mybir.dt.bfloat16, mybir.dt.float32, mybir.dt.uint16
+ALU = mybir.AluOpType
+ACT = mybir.ActivationFunctionType
+
+P = 128
+CHANNELS = 512
+HEADS = CHANNELS // P
+TOKENS = 2048
+PLACES = 256
+HALVES = PLACES // P
+SLOTS = 4096
+GROUP = 512
+GROUPS = TOKENS // GROUP
+SAMPLES_PER_GROUP = GROUP // PLACES
+MASKED = -30000.0
+
+FLOPS = 4 * 2 * CHANNELS * CHANNELS * TOKENS + 2 * 2 * (TOKENS // PLACES) * HEADS * P * PLACES * PLACES
+
+
+def block(i, size=P):
+    return slice(i * size, (i + 1) * size)
+
+
+def tile_t2gformer_mae_b_kernel(
+    tc, base, x_head, x_tail, w_head, b_head, w_v, b_v, w_out, b_out, rel, topo, offs, out
+):
+    nc = tc.nc
+    with (
+        tc.tile_pool(name="held", bufs=1) as held,
+        tc.tile_pool(name="inputs", bufs=GROUPS) as inputs,
+        tc.tile_pool(name="projected", bufs=3) as projected,
+        tc.tile_pool(name="values", bufs=2) as values,
+        tc.tile_pool(name="softmax", bufs=3) as softmax,
+        tc.tile_pool(name="results", bufs=2) as results,
+        tc.psum_pool(name="psum_proj", bufs=2) as psum_proj,
+        tc.psum_pool(name="psum_score", bufs=2) as psum_score,
+        tc.psum_pool(name="psum_flip", bufs=2) as psum_flip,
+        tc.psum_pool(name="psum_att", bufs=2) as psum_att,
+    ):
+        offsets = held.tile([P, TOKENS // 16], U16, name="offsets")
+        nc.sync.dma_start(offsets[:], offs)
+
+        def load_weights(w, name):
+            w_sb = held.tile([P, HEADS, CHANNELS], BF16, name=name)
+            nc.sync.dma_start(w_sb[:], w.rearrange("(a p) c -> p a c", p=P))
+            return w_sb
+
+        def load_tokens(x, g, name):
+            x_sb = inputs.tile([P, HEADS, GROUP], BF16, name=name)
+            nc.sync.dma_start(x_sb[:], x.rearrange("(a p) n -> p a n", p=P)[:, :, block(g, GROUP)])
+            return x_sb
+
+        xt_sb = [load_tokens(x_tail, 0, "xt_sb")]
+        w_v_sb = load_weights(w_v, "w_v_sb")
+        w_head_sb = load_weights(w_head, "w_head_sb")
+        xh_sb = [load_tokens(x_head, 0, "xh_sb")]
+        for g in range(1, GROUPS):
+            xt_sb.append(load_tokens(x_tail, g, "xt_sb"))
+            xh_sb.append(load_tokens(x_head, g, "xh_sb"))
+        w_out_sb = load_weights(w_out, "w_out_sb")
+        windows = [held.tile([P, SLOTS], F32, name=f"window{c}") for c in range(HEADS)]
+        for c in range(HEADS):
+            nc.sync.dma_start(windows[c][:], base[block(c), :])
+
+        vector_rows = held.tile([P, P], F32, name="vector_rows")
+        nc.vector.memset(vector_rows[:], 0.0)
+        for r, v in enumerate((b_head, rel, b_v, b_out)):
+            nc.scalar.dma_start(vector_rows[block(r, HEADS), :], v.rearrange("(a p) o -> a (p o)", p=P))
+        topo_sb = held.tile([P, HEADS, HALVES, PLACES], F32, name="topo_sb")
+        nc.scalar.dma_start(topo_sb[:], topo.rearrange("h (a p) i -> p h a i", p=P))
+
+        identity_f32 = held.tile([P, P], F32, name="identity_f32")
+        make_identity(nc, identity_f32[:])
+        identity = held.tile([P, P], BF16, name="identity")
+        make_identity(nc, identity[:])
+
+        columns_ps = psum_proj.tile([P, GROUP], F32, name="proj_ps")
+        nc.tensor.transpose(columns_ps[:, 0:P], vector_rows[:], identity_f32[:])
+        columns = held.tile([P, 4 * HEADS], F32, name="columns")
+        nc.vector.tensor_copy(columns[:], columns_ps[:, 0 : 4 * HEADS])
+        b_head_col, rel_col, b_v_col, b_out_col = [columns[:, block(r, HEADS)] for r in range(4)]
+        q_scale = held.tile([P, HEADS], F32, name="q_scale")
+        nc.vector.tensor_scalar_mul(q_scale[:], rel_col, 1.0 / math.sqrt(P))
+        q_bias = held.tile([P, HEADS], F32, name="q_bias")
+        nc.vector.tensor_mul(q_bias[:], b_head_col, q_scale[:])
+
+        def flip_256(out_ps, in_sb):
+            for x, y in product(range(HALVES), range(HALVES)):
+                nc.tensor.transpose(out_ps[:, x, block(y)], in_sb[:, y, block(x)], identity[:])
+
+        never = held.tile([P, HALVES, PLACES], BF16, name="never")
+        nc.vector.memset(never[:], 0.0)
+        for c in range(HALVES):
+            nc.vector.tensor_scalar_mul(never[:, c, block(c)], identity[:], MASKED)
+        nc.vector.memset(never[:, :, 0:1], MASKED)
+        mask_ti = held.tile([P, HEADS, HALVES, PLACES], BF16, name="mask_ti")
+        nc.vector.tensor_scalar(mask_ti[:], topo_sb[:], 1.0, -MASKED, ALU.subtract, ALU.mult)
+        mask = held.tile([P, HEADS, HALVES, PLACES], BF16, name="mask")
+        for h in range(HEADS):
+            mask_ps = psum_flip.tile([P, HALVES, PLACES], BF16, name="flip_ps")
+            flip_256(mask_ps, mask_ti[:, h])
+            nc.vector.tensor_tensor(mask[:, h], mask_ps[:], never[:], ALU.add)
+
+        zeros = held.tile([P, TOKENS], F32, name="zeros")
+        nc.gpsimd.memset(zeros[:], 0.0)
+        b_out_wide = [held.tile([P, TOKENS], F32, name=f"b_out_wide{c}") for c in range(HEADS)]
+        for c in range(HEADS):
+            nc.vector.tensor_scalar_add(b_out_wide[c][:], zeros[:], b_out_col[:, c : c + 1])
+
+        att_sb = held.tile([P, HEADS, TOKENS], BF16, name="att_sb")
+
+        def project(w_sb, c, x_sb):
+            proj_ps = psum_proj.tile([P, GROUP], F32, name="proj_ps")
+            for k in range(HEADS):
+                nc.tensor.matmul(
+                    proj_ps[:], w_sb[:, k, block(c)], x_sb[:, k, :], start=(k == 0), stop=(k == HEADS - 1)
+                )
+            return proj_ps
+
+        def attend(q_sb, k_sb, fv_sb, h, s, att_ps):
+            score_ps = psum_score.tile([P, HALVES, PLACES], F32, name="score_ps")
+            for c in range(HALVES):
+                nc.tensor.matmul(
+                    score_ps[:, c, :], q_sb[:, block(HALVES * s + c)], k_sb[:, block(s, PLACES)], start=True, stop=True
+                )
+            score = softmax.tile([P, HALVES, PLACES], F32, name="score")
+            nc.vector.tensor_tensor(score[:], score_ps[:], mask[:, h], ALU.add)
+            minus_max = softmax.tile([P, HALVES], F32, name="minus_max")
+            nc.vector.reduce_max(minus_max[:], score[:], axis=mybir.AxisListType.X, negate=True)
+            e = softmax.tile([P, HALVES, PLACES], F32, name="e")
+            e_sum = softmax.tile([P, HALVES], F32, name="e_sum")
+            for c in range(HALVES):
+                nc.scalar.activation(
+                    e[:, c, :], score[:, c, :], ACT.Exp, bias=minus_max[:, c : c + 1], accum_out=e_sum[:, c : c + 1]
+                )
+            one_over_sum = softmax.tile([P, HALVES], F32, name="one_over_sum")
+            nc.vector.reciprocal(one_over_sum[:], e_sum[:])
+            p = softmax.tile([P, HALVES, PLACES], BF16, name="p")
+            for c in range(HALVES):
+                nc.vector.tensor_scalar_mul(p[:, c, :], e[:, c, :], one_over_sum[:, c : c + 1])
+            p_flipped_ps = psum_flip.tile([P, HALVES, PLACES], BF16, name="flip_ps")
+            flip_256(p_flipped_ps, p)
+            p_flipped = softmax.tile([P, HALVES, PLACES], BF16, name="p_flipped")
+            nc.vector.tensor_copy(p_flipped[:], p_flipped_ps[:])
+            for a in range(HALVES):
+                nc.tensor.matmul(
+                    att_ps[:, block(s, PLACES)],
+                    fv_sb[:, HALVES * s + a, block(h)],
+                    p_flipped[:, a, :],
+                    start=(a == 0),
+                    stop=(a == HALVES - 1),
+                )
+
+        def project_out(c, g, y_sb):
+            y_ps = project(w_out_sb, c, att_sb[:, :, block(g, GROUP)])
+            nc.scalar.copy(y_sb[:, block(g, GROUP)], y_ps[:])
+
+        def place(c, y_sb):
+            nc.vector.tensor_tensor(windows[c][:].indirect(offsets[:]), y_sb[:], b_out_wide[c][:], ALU.add)
+            nc.sync.dma_start(out[block(c), :], windows[c][:])
+
+        y_first = results.tile([P, TOKENS], F32, name="y_sb")
+        for g in range(GROUPS):
+            fv_sb = values.tile([P, GROUP // P, CHANNELS], BF16, name="fv_sb")
+            for j in range(GROUP // P):
+                fv_ps = psum_proj.tile([P, CHANNELS], F32, name="proj_ps")
+                for k in range(HEADS):
+                    nc.tensor.matmul(
+                        fv_ps[:], xt_sb[g][:, k, block(j)], w_v_sb[:, k, :], start=(k == 0), stop=(k == HEADS - 1)
+                    )
+                nc.scalar.copy(fv_sb[:, j, :], fv_ps[:])
+            for h in range(HEADS):
+                q_sb = projected.tile([P, GROUP], BF16, name="q_sb")
+                nc.scalar.activation(
+                    q_sb[:],
+                    project(w_head_sb, h, xh_sb[g])[:],
+                    ACT.Identity,
+                    bias=q_bias[:, h : h + 1],
+                    scale=q_scale[:, h : h + 1],
+                )
+                k_sb = projected.tile([P, GROUP], BF16, name="k_sb")
+                nc.scalar.activation(
+                    k_sb[:], project(w_head_sb, h, xt_sb[g])[:], ACT.Identity, bias=b_head_col[:, h : h + 1]
+                )
+                att_ps = psum_att.tile([P, GROUP], F32, name="att_ps")
+                for s in range(SAMPLES_PER_GROUP):
+                    attend(q_sb, k_sb, fv_sb, h, s, att_ps)
+                nc.scalar.activation(
+                    att_sb[:, h, block(g, GROUP)], att_ps[:], ACT.Identity, bias=b_v_col[:, h : h + 1]
+                )
+            project_out(0, g, y_first)
+        place(0, y_first)
+        for c in range(1, HEADS):
+            y_sb = results.tile([P, TOKENS], F32, name="y_sb")
+            for g in range(GROUPS):
+                project_out(c, g, y_sb)
+            place(c, y_sb)

@@ -35,8 +35,9 @@ def tile_t2gformer_mae_b_kernel(
         tc.tile_pool(name="held", bufs=1) as held,
         tc.tile_pool(name="inputs", bufs=GROUPS) as inputs,
         tc.tile_pool(name="projected", bufs=3) as projected,
-        tc.tile_pool(name="values", bufs=2) as values,
+        tc.tile_pool(name="values", bufs=2 * GROUP // P) as values,
         tc.tile_pool(name="softmax", bufs=3) as softmax,
+        tc.tile_pool(name="weights", bufs=4) as weights,
         tc.tile_pool(name="results", bufs=2) as results,
         tc.psum_pool(name="psum_proj", bufs=2) as psum_proj,
         tc.psum_pool(name="psum_score", bufs=2) as psum_score,
@@ -48,47 +49,40 @@ def tile_t2gformer_mae_b_kernel(
 
         def load_weights(w, name):
             w_sb = held.tile([P, HEADS, CHANNELS], BF16, name=name)
-            nc.sync.dma_start(w_sb[:], w.rearrange("(a p) c -> p a c", p=P))
+            for k in range(HEADS):
+                nc.scalar.dma_start(w_sb[:, k, :], w[block(k), :])
             return w_sb
 
         def load_tokens(x, g, name):
             x_sb = inputs.tile([P, HEADS, GROUP], BF16, name=name)
-            nc.sync.dma_start(x_sb[:], x.rearrange("(a p) n -> p a n", p=P)[:, :, block(g, GROUP)])
+            for k in range(HEADS):
+                nc.sync.dma_start(x_sb[:, k, :], x[block(k), block(g, GROUP)])
             return x_sb
-
-        xt_sb = [load_tokens(x_tail, 0, "xt_sb")]
-        w_v_sb = load_weights(w_v, "w_v_sb")
-        w_head_sb = load_weights(w_head, "w_head_sb")
-        xh_sb = [load_tokens(x_head, 0, "xh_sb")]
-        for g in range(1, GROUPS):
-            xt_sb.append(load_tokens(x_tail, g, "xt_sb"))
-            xh_sb.append(load_tokens(x_head, g, "xh_sb"))
-        w_out_sb = load_weights(w_out, "w_out_sb")
-        windows = [held.tile([P, SLOTS], F32, name=f"window{c}") for c in range(HEADS)]
-        for c in range(HEADS):
-            nc.sync.dma_start(windows[c][:], base[block(c), :])
 
         vector_rows = held.tile([P, P], F32, name="vector_rows")
         nc.vector.memset(vector_rows[:], 0.0)
         for r, v in enumerate((b_head, rel, b_v, b_out)):
             nc.scalar.dma_start(vector_rows[block(r, HEADS), :], v.rearrange("(a p) o -> a (p o)", p=P))
+        w_v_sb = load_weights(w_v, "w_v_sb")
+        w_head_sb = load_weights(w_head, "w_head_sb")
+        w_out_sb = load_weights(w_out, "w_out_sb")
+
+        xt_sb = [load_tokens(x_tail, 0, "xt_sb")]
+        xh_sb = [load_tokens(x_head, 0, "xh_sb")]
         topo_sb = held.tile([P, HEADS, HALVES, PLACES], F32, name="topo_sb")
-        nc.scalar.dma_start(topo_sb[:], topo.rearrange("h (a p) i -> p h a i", p=P))
+        for h in range(HEADS):
+            nc.sync.dma_start(topo_sb[:, h], topo[h].rearrange("(a p) i -> p a i", p=P))
+        for g in range(1, GROUPS):
+            xt_sb.append(load_tokens(x_tail, g, "xt_sb"))
+            xh_sb.append(load_tokens(x_head, g, "xh_sb"))
+        windows = [held.tile([P, SLOTS], F32, name=f"window{c}") for c in range(HEADS)]
+        for c in range(HEADS):
+            nc.sync.dma_start(windows[c][:], base[block(c), :])
 
         identity_f32 = held.tile([P, P], F32, name="identity_f32")
         make_identity(nc, identity_f32[:])
         identity = held.tile([P, P], BF16, name="identity")
         make_identity(nc, identity[:])
-
-        columns_ps = psum_proj.tile([P, GROUP], F32, name="proj_ps")
-        nc.tensor.transpose(columns_ps[:, 0:P], vector_rows[:], identity_f32[:])
-        columns = held.tile([P, 4 * HEADS], F32, name="columns")
-        nc.vector.tensor_copy(columns[:], columns_ps[:, 0 : 4 * HEADS])
-        b_head_col, rel_col, b_v_col, b_out_col = [columns[:, block(r, HEADS)] for r in range(4)]
-        q_scale = held.tile([P, HEADS], F32, name="q_scale")
-        nc.vector.tensor_scalar_mul(q_scale[:], rel_col, 1.0 / math.sqrt(P))
-        q_bias = held.tile([P, HEADS], F32, name="q_bias")
-        nc.vector.tensor_mul(q_bias[:], b_head_col, q_scale[:])
 
         def flip_256(out_ps, in_sb):
             for x, y in product(range(HALVES), range(HALVES)):
@@ -100,18 +94,30 @@ def tile_t2gformer_mae_b_kernel(
             nc.vector.tensor_scalar_mul(never[:, c, block(c)], identity[:], MASKED)
         nc.vector.memset(never[:, :, 0:1], MASKED)
         mask_ti = held.tile([P, HEADS, HALVES, PLACES], BF16, name="mask_ti")
-        nc.vector.tensor_scalar(mask_ti[:], topo_sb[:], 1.0, -MASKED, ALU.subtract, ALU.mult)
         mask = held.tile([P, HEADS, HALVES, PLACES], BF16, name="mask")
-        for h in range(HEADS):
+
+        def make_mask(h):
+            nc.vector.tensor_scalar(mask_ti[:, h], topo_sb[:, h], 1.0, -MASKED, ALU.subtract, ALU.mult)
             mask_ps = psum_flip.tile([P, HALVES, PLACES], BF16, name="flip_ps")
             flip_256(mask_ps, mask_ti[:, h])
             nc.vector.tensor_tensor(mask[:, h], mask_ps[:], never[:], ALU.add)
 
+        columns = held.tile([P, 4 * HEADS], F32, name="columns")
+        b_head_col, rel_col, b_v_col, b_out_col = [columns[:, block(r, HEADS)] for r in range(4)]
+        q_scale = held.tile([P, HEADS], F32, name="q_scale")
+        q_bias = held.tile([P, HEADS], F32, name="q_bias")
         zeros = held.tile([P, TOKENS], F32, name="zeros")
         nc.gpsimd.memset(zeros[:], 0.0)
         b_out_wide = [held.tile([P, TOKENS], F32, name=f"b_out_wide{c}") for c in range(HEADS)]
-        for c in range(HEADS):
-            nc.vector.tensor_scalar_add(b_out_wide[c][:], zeros[:], b_out_col[:, c : c + 1])
+
+        def spread_vectors():
+            columns_ps = psum_proj.tile([P, GROUP], F32, name="proj_ps")
+            nc.tensor.transpose(columns_ps[:, 0:P], vector_rows[:], identity_f32[:])
+            nc.vector.tensor_copy(columns[:], columns_ps[:, 0 : 4 * HEADS])
+            nc.vector.tensor_scalar_mul(q_scale[:], rel_col, 1.0 / math.sqrt(P))
+            nc.vector.tensor_mul(q_bias[:], b_head_col, q_scale[:])
+            for c in range(HEADS):
+                nc.gpsimd.tensor_scalar(b_out_wide[c][:], zeros[:], b_out_col[:, c : c + 1], 1.0, ALU.add, ALU.mult)
 
         att_sb = held.tile([P, HEADS, TOKENS], BF16, name="att_sb")
 
@@ -123,7 +129,35 @@ def tile_t2gformer_mae_b_kernel(
                 )
             return proj_ps
 
-        def attend(q_sb, k_sb, fv_sb, h, s, att_ps):
+        def project_q(g, h):
+            q_sb = projected.tile([P, GROUP], BF16, name="q_sb")
+            nc.scalar.activation(
+                q_sb[:],
+                project(w_head_sb, h, xh_sb[g])[:],
+                ACT.Identity,
+                bias=q_bias[:, h : h + 1],
+                scale=q_scale[:, h : h + 1],
+            )
+            return q_sb
+
+        def project_k(g, h):
+            k_sb = projected.tile([P, GROUP], BF16, name="k_sb")
+            nc.scalar.activation(
+                k_sb[:], project(w_head_sb, h, xt_sb[g])[:], ACT.Identity, bias=b_head_col[:, h : h + 1]
+            )
+            return k_sb
+
+        def project_values(g, j):
+            fv_ps = psum_proj.tile([P, CHANNELS], F32, name="proj_ps")
+            for k in range(HEADS):
+                nc.tensor.matmul(
+                    fv_ps[:], xt_sb[g][:, k, block(j)], w_v_sb[:, k, :], start=(k == 0), stop=(k == HEADS - 1)
+                )
+            fv_sb = values.tile([P, CHANNELS], BF16, name="fv_sb")
+            nc.scalar.copy(fv_sb[:], fv_ps[:])
+            return fv_sb
+
+        def scores_to_exp(q_sb, k_sb, h, s):
             score_ps = psum_score.tile([P, HALVES, PLACES], F32, name="score_ps")
             for c in range(HALVES):
                 nc.tensor.matmul(
@@ -139,23 +173,36 @@ def tile_t2gformer_mae_b_kernel(
                 nc.scalar.activation(
                     e[:, c, :], score[:, c, :], ACT.Exp, bias=minus_max[:, c : c + 1], accum_out=e_sum[:, c : c + 1]
                 )
+            return e, e_sum
+
+        def normalise(e, e_sum):
             one_over_sum = softmax.tile([P, HALVES], F32, name="one_over_sum")
             nc.vector.reciprocal(one_over_sum[:], e_sum[:])
-            p = softmax.tile([P, HALVES, PLACES], BF16, name="p")
+            p = weights.tile([P, HALVES, PLACES], BF16, name="p")
             for c in range(HALVES):
                 nc.vector.tensor_scalar_mul(p[:, c, :], e[:, c, :], one_over_sum[:, c : c + 1])
+            return p
+
+        def flip(p):
             p_flipped_ps = psum_flip.tile([P, HALVES, PLACES], BF16, name="flip_ps")
             flip_256(p_flipped_ps, p)
-            p_flipped = softmax.tile([P, HALVES, PLACES], BF16, name="p_flipped")
+            p_flipped = weights.tile([P, HALVES, PLACES], BF16, name="p_flipped")
             nc.vector.tensor_copy(p_flipped[:], p_flipped_ps[:])
-            for a in range(HALVES):
-                nc.tensor.matmul(
-                    att_ps[:, block(s, PLACES)],
-                    fv_sb[:, HALVES * s + a, block(h)],
-                    p_flipped[:, a, :],
-                    start=(a == 0),
-                    stop=(a == HALVES - 1),
-                )
+            return p_flipped
+
+        def weighted_sums(g, h, fv_sb, p_of_sample):
+            flipped = [flip(p) for p in p_of_sample]
+            att_ps = psum_att.tile([P, GROUP], F32, name="att_ps")
+            for s in range(SAMPLES_PER_GROUP):
+                for a in range(HALVES):
+                    nc.tensor.matmul(
+                        att_ps[:, block(s, PLACES)],
+                        fv_sb[HALVES * s + a][:, block(h)],
+                        flipped[s][:, a, :],
+                        start=(a == 0),
+                        stop=(a == HALVES - 1),
+                    )
+            nc.scalar.activation(att_sb[:, h, block(g, GROUP)], att_ps[:], ACT.Identity, bias=b_v_col[:, h : h + 1])
 
         def project_out(c, g, y_sb):
             y_ps = project(w_out_sb, c, att_sb[:, :, block(g, GROUP)])
@@ -166,35 +213,41 @@ def tile_t2gformer_mae_b_kernel(
             nc.sync.dma_start(out[block(c), :], windows[c][:])
 
         y_first = results.tile([P, TOKENS], F32, name="y_sb")
-        for g in range(GROUPS):
-            fv_sb = values.tile([P, GROUP // P, CHANNELS], BF16, name="fv_sb")
-            for j in range(GROUP // P):
-                fv_ps = psum_proj.tile([P, CHANNELS], F32, name="proj_ps")
-                for k in range(HEADS):
-                    nc.tensor.matmul(
-                        fv_ps[:], xt_sb[g][:, k, block(j)], w_v_sb[:, k, :], start=(k == 0), stop=(k == HEADS - 1)
-                    )
-                nc.scalar.copy(fv_sb[:, j, :], fv_ps[:])
-            for h in range(HEADS):
-                q_sb = projected.tile([P, GROUP], BF16, name="q_sb")
-                nc.scalar.activation(
-                    q_sb[:],
-                    project(w_head_sb, h, xh_sb[g])[:],
-                    ACT.Identity,
-                    bias=q_bias[:, h : h + 1],
-                    scale=q_scale[:, h : h + 1],
-                )
-                k_sb = projected.tile([P, GROUP], BF16, name="k_sb")
-                nc.scalar.activation(
-                    k_sb[:], project(w_head_sb, h, xt_sb[g])[:], ACT.Identity, bias=b_head_col[:, h : h + 1]
-                )
-                att_ps = psum_att.tile([P, GROUP], F32, name="att_ps")
-                for s in range(SAMPLES_PER_GROUP):
-                    attend(q_sb, k_sb, fv_sb, h, s, att_ps)
-                nc.scalar.activation(
-                    att_sb[:, h, block(g, GROUP)], att_ps[:], ACT.Identity, bias=b_v_col[:, h : h + 1]
-                )
-            project_out(0, g, y_first)
+        steps = list(product(range(GROUPS), range(HEADS)))
+
+        def finish(step, fv_sb, p_of_sample):
+            g, h = step
+            weighted_sums(g, h, fv_sb, p_of_sample)
+            if h == HEADS - 1:
+                project_out(0, g, y_first)
+
+        fv_of_group = {g: [] for g in range(GROUPS)}
+        for j in range(GROUP // P):
+            fv_of_group[0].append(project_values(0, j))
+        spread_vectors()
+        q_sb, k_sb = project_q(0, 0), project_k(0, 0)
+        make_mask(0)
+        unfinished = None
+        for n, (g, h) in enumerate(steps):
+            following = steps[n + 1] if n + 1 < len(steps) else None
+            e_0 = scores_to_exp(q_sb, k_sb, h, 0)
+            if following:
+                q_next = project_q(*following)
+            e_1 = scores_to_exp(q_sb, k_sb, h, 1)
+            if following:
+                k_next = project_k(*following)
+            if g == 0 and h + 1 < HEADS:
+                make_mask(h + 1)
+            p_0 = normalise(*e_0)
+            if g + 1 < GROUPS:
+                fv_of_group[g + 1].append(project_values(g + 1, h))
+            p_1 = normalise(*e_1)
+            if unfinished:
+                finish(*unfinished)
+            unfinished = ((g, h), fv_of_group[g], [p_0, p_1])
+            q_sb, k_sb = q_next, k_next
+        finish(*unfinished)
+
         place(0, y_first)
         for c in range(1, HEADS):
             y_sb = results.tile([P, TOKENS], F32, name="y_sb")

@@ -44,31 +44,28 @@ def tile_t2gformer_mae_b_kernel(
         tc.psum_pool(name="psum_flip", bufs=2) as psum_flip,
         tc.psum_pool(name="psum_att", bufs=2) as psum_att,
     ):
-        offsets = held.tile([P, TOKENS // 16], U16, name="offsets")
-        nc.sync.dma_start(offsets[:], offs)
-
-        def load_weights(w, name):
+        def load_weights(queue, w, name):
             w_sb = held.tile([P, HEADS, CHANNELS], BF16, name=name)
-            for k in range(HEADS):
-                nc.scalar.dma_start(w_sb[:, k, :], w[block(k), :])
+            queue.dma_start(w_sb[:], w.rearrange("(a p) c -> p a c", p=P))
             return w_sb
 
         def load_tokens(x, g, name):
             x_sb = inputs.tile([P, HEADS, GROUP], BF16, name=name)
-            for k in range(HEADS):
-                nc.sync.dma_start(x_sb[:, k, :], x[block(k), block(g, GROUP)])
+            nc.sync.dma_start(x_sb[:], x.rearrange("(a p) n -> p a n", p=P)[:, :, block(g, GROUP)])
             return x_sb
 
+        w_v_sb = load_weights(nc.scalar, w_v, "w_v_sb")
+        w_head_sb = load_weights(nc.scalar, w_head, "w_head_sb")
         vector_rows = held.tile([P, P], F32, name="vector_rows")
-        nc.vector.memset(vector_rows[:], 0.0)
+        nc.gpsimd.memset(vector_rows[:], 0.0)
         for r, v in enumerate((b_head, rel, b_v, b_out)):
-            nc.scalar.dma_start(vector_rows[block(r, HEADS), :], v.rearrange("(a p) o -> a (p o)", p=P))
-        w_v_sb = load_weights(w_v, "w_v_sb")
-        w_head_sb = load_weights(w_head, "w_head_sb")
-        w_out_sb = load_weights(w_out, "w_out_sb")
+            nc.gpsimd.dma_start(vector_rows[block(r, HEADS), :], v.rearrange("(a p) o -> a (p o)", p=P))
+        w_out_sb = load_weights(nc.gpsimd, w_out, "w_out_sb")
 
         xt_sb = [load_tokens(x_tail, 0, "xt_sb")]
         xh_sb = [load_tokens(x_head, 0, "xh_sb")]
+        offsets = held.tile([P, TOKENS // 16], U16, name="offsets")
+        nc.sync.dma_start(offsets[:], offs)
         topo_sb = held.tile([P, HEADS, HALVES, PLACES], F32, name="topo_sb")
         for h in range(HEADS):
             nc.sync.dma_start(topo_sb[:, h], topo[h].rearrange("(a p) i -> p a i", p=P))
@@ -190,8 +187,8 @@ def tile_t2gformer_mae_b_kernel(
             nc.vector.tensor_copy(p_flipped[:], p_flipped_ps[:])
             return p_flipped
 
-        def weighted_sums(g, h, fv_sb, p_of_sample):
-            flipped = [flip(p) for p in p_of_sample]
+        def weighted_sums(g, h, flipped):
+            fv_sb = fv_of_group[g]
             att_ps = psum_att.tile([P, GROUP], F32, name="att_ps")
             for s in range(SAMPLES_PER_GROUP):
                 for a in range(HALVES):
@@ -214,39 +211,33 @@ def tile_t2gformer_mae_b_kernel(
 
         y_first = results.tile([P, TOKENS], F32, name="y_sb")
         steps = list(product(range(GROUPS), range(HEADS)))
-
-        def finish(step, fv_sb, p_of_sample):
-            g, h = step
-            weighted_sums(g, h, fv_sb, p_of_sample)
-            if h == HEADS - 1:
-                project_out(0, g, y_first)
-
         fv_of_group = {g: [] for g in range(GROUPS)}
         for j in range(GROUP // P):
             fv_of_group[0].append(project_values(0, j))
         spread_vectors()
         q_sb, k_sb = project_q(0, 0), project_k(0, 0)
         make_mask(0)
-        unfinished = None
         for n, (g, h) in enumerate(steps):
-            following = steps[n + 1] if n + 1 < len(steps) else None
             e_0 = scores_to_exp(q_sb, k_sb, h, 0)
-            if following:
-                q_next = project_q(*following)
+            if n + 1 < len(steps):
+                q_next = project_q(*steps[n + 1])
             e_1 = scores_to_exp(q_sb, k_sb, h, 1)
-            if following:
-                k_next = project_k(*following)
+            if n + 1 < len(steps):
+                k_next = project_k(*steps[n + 1])
             if g == 0 and h + 1 < HEADS:
                 make_mask(h + 1)
-            p_0 = normalise(*e_0)
+            if n > 0:
+                flipped = [flip(p) for p in p_of_sample]
             if g + 1 < GROUPS:
                 fv_of_group[g + 1].append(project_values(g + 1, h))
-            p_1 = normalise(*e_1)
-            if unfinished:
-                finish(*unfinished)
-            unfinished = ((g, h), fv_of_group[g], [p_0, p_1])
+            if n > 0:
+                weighted_sums(*steps[n - 1], flipped)
+            p_of_sample = [normalise(*e_0), normalise(*e_1)]
             q_sb, k_sb = q_next, k_next
-        finish(*unfinished)
+        for g in range(GROUPS - 1):
+            project_out(0, g, y_first)
+        weighted_sums(*steps[-1], [flip(p) for p in p_of_sample])
+        project_out(0, GROUPS - 1, y_first)
 
         place(0, y_first)
         for c in range(1, HEADS):

@@ -39,10 +39,10 @@ def tile_t2gformer_mae_b_kernel(
         tc.tile_pool(name="softmax", bufs=3) as softmax,
         tc.tile_pool(name="weights", bufs=4) as weights,
         tc.tile_pool(name="results", bufs=2) as results,
-        tc.psum_pool(name="psum_proj", bufs=2) as psum_proj,
+        tc.psum_pool(name="psum_proj", bufs=3) as psum_proj,
         tc.psum_pool(name="psum_score", bufs=2) as psum_score,
         tc.psum_pool(name="psum_flip", bufs=2) as psum_flip,
-        tc.psum_pool(name="psum_att", bufs=2) as psum_att,
+        tc.psum_pool(name="psum_att", bufs=1) as psum_att,
     ):
         def load_weights(queue, w, name):
             w_sb = held.tile([P, HEADS, CHANNELS], BF16, name=name)
@@ -154,12 +154,15 @@ def tile_t2gformer_mae_b_kernel(
             nc.scalar.copy(fv_sb[:], fv_ps[:])
             return fv_sb
 
-        def scores_to_exp(q_sb, k_sb, h, s):
+        def scores(q_sb, k_sb, s):
             score_ps = psum_score.tile([P, HALVES, PLACES], F32, name="score_ps")
             for c in range(HALVES):
                 nc.tensor.matmul(
                     score_ps[:, c, :], q_sb[:, block(HALVES * s + c)], k_sb[:, block(s, PLACES)], start=True, stop=True
                 )
+            return score_ps
+
+        def exponentials(score_ps, h):
             score = softmax.tile([P, HALVES, PLACES], F32, name="score")
             nc.vector.tensor_tensor(score[:], score_ps[:], mask[:, h], ALU.add)
             minus_max = softmax.tile([P, HALVES], F32, name="minus_max")
@@ -218,12 +221,14 @@ def tile_t2gformer_mae_b_kernel(
         q_sb, k_sb = project_q(0, 0), project_k(0, 0)
         make_mask(0)
         for n, (g, h) in enumerate(steps):
-            e_0 = scores_to_exp(q_sb, k_sb, h, 0)
+            score_0 = scores(q_sb, k_sb, 0)
             if n + 1 < len(steps):
                 q_next = project_q(*steps[n + 1])
-            e_1 = scores_to_exp(q_sb, k_sb, h, 1)
+            e_0 = exponentials(score_0, h)
+            score_1 = scores(q_sb, k_sb, 1)
             if n + 1 < len(steps):
                 k_next = project_k(*steps[n + 1])
+            e_1 = exponentials(score_1, h)
             if g == 0 and h + 1 < HEADS:
                 make_mask(h + 1)
             if n > 0:

@@ -44,42 +44,44 @@ def tile_t2gformer_mae_b_kernel(
         tc.psum_pool(name="psum_flip", bufs=2) as psum_flip,
         tc.psum_pool(name="psum_att", bufs=1) as psum_att,
     ):
+        identity = held.tile([P, P], BF16, name="identity")
+        make_identity(nc, identity[:])
+
         def load_weights(queue, w, name):
             w_sb = held.tile([P, HEADS, CHANNELS], BF16, name=name)
             queue.dma_start(w_sb[:], w.rearrange("(a p) c -> p a c", p=P))
             return w_sb
 
-        def load_tokens(x, g, name):
+        def load_tokens(queue, x, g, name):
             x_sb = inputs.tile([P, HEADS, GROUP], BF16, name=name)
-            nc.sync.dma_start(x_sb[:], x.rearrange("(a p) n -> p a n", p=P)[:, :, block(g, GROUP)])
+            queue.dma_start(x_sb[:], x.rearrange("(a p) n -> p a n", p=P)[:, :, block(g, GROUP)])
             return x_sb
 
-        w_v_sb = load_weights(nc.scalar, w_v, "w_v_sb")
-        w_head_sb = load_weights(nc.scalar, w_head, "w_head_sb")
-        vector_rows = held.tile([P, P], F32, name="vector_rows")
-        nc.gpsimd.memset(vector_rows[:], 0.0)
-        for r, v in enumerate((b_head, rel, b_v, b_out)):
-            nc.gpsimd.dma_start(vector_rows[block(r, HEADS), :], v.rearrange("(a p) o -> a (p o)", p=P))
-        w_out_sb = load_weights(nc.gpsimd, w_out, "w_out_sb")
+        def load_column(queue, v, name):
+            column = held.tile([P, HEADS], F32, name=name)
+            queue.dma_start(column[:], v.rearrange("(a p) o -> p (a o)", p=P))
+            return column
 
-        xt_sb = [load_tokens(x_tail, 0, "xt_sb")]
-        xh_sb = [load_tokens(x_head, 0, "xh_sb")]
+        w_head_sb = load_weights(nc.sync, w_head, "w_head_sb")
+        xh_sb = [load_tokens(nc.scalar, x_head, 0, "xh_sb")]
+        xt_sb = [load_tokens(nc.sync, x_tail, 0, "xt_sb")]
+        rel_col = load_column(nc.scalar, rel, "rel_col")
+        b_head_col = load_column(nc.scalar, b_head, "b_head_col")
+        w_v_sb = load_weights(nc.scalar, w_v, "w_v_sb")
         offsets = held.tile([P, TOKENS // 16], U16, name="offsets")
         nc.sync.dma_start(offsets[:], offs)
         topo_sb = held.tile([P, HEADS, HALVES, PLACES], F32, name="topo_sb")
         for h in range(HEADS):
             nc.sync.dma_start(topo_sb[:, h], topo[h].rearrange("(a p) i -> p a i", p=P))
+        b_v_col = load_column(nc.sync, b_v, "b_v_col")
+        b_out_col = load_column(nc.sync, b_out, "b_out_col")
         for g in range(1, GROUPS):
-            xt_sb.append(load_tokens(x_tail, g, "xt_sb"))
-            xh_sb.append(load_tokens(x_head, g, "xh_sb"))
+            xt_sb.append(load_tokens(nc.sync, x_tail, g, "xt_sb"))
+            xh_sb.append(load_tokens(nc.sync, x_head, g, "xh_sb"))
+        w_out_sb = load_weights(nc.sync, w_out, "w_out_sb")
         windows = [held.tile([P, SLOTS], F32, name=f"window{c}") for c in range(HEADS)]
         for c in range(HEADS):
             nc.sync.dma_start(windows[c][:], base[block(c), :])
-
-        identity_f32 = held.tile([P, P], F32, name="identity_f32")
-        make_identity(nc, identity_f32[:])
-        identity = held.tile([P, P], BF16, name="identity")
-        make_identity(nc, identity[:])
 
         def flip_256(out_ps, in_sb):
             for x, y in product(range(HALVES), range(HALVES)):
@@ -99,8 +101,6 @@ def tile_t2gformer_mae_b_kernel(
             flip_256(mask_ps, mask_ti[:, h])
             nc.vector.tensor_tensor(mask[:, h], mask_ps[:], never[:], ALU.add)
 
-        columns = held.tile([P, 4 * HEADS], F32, name="columns")
-        b_head_col, rel_col, b_v_col, b_out_col = [columns[:, block(r, HEADS)] for r in range(4)]
         q_scale = held.tile([P, HEADS], F32, name="q_scale")
         q_bias = held.tile([P, HEADS], F32, name="q_bias")
         zeros = held.tile([P, TOKENS], F32, name="zeros")
@@ -108,11 +108,8 @@ def tile_t2gformer_mae_b_kernel(
         b_out_wide = [held.tile([P, TOKENS], F32, name=f"b_out_wide{c}") for c in range(HEADS)]
 
         def spread_vectors():
-            columns_ps = psum_proj.tile([P, GROUP], F32, name="proj_ps")
-            nc.tensor.transpose(columns_ps[:, 0:P], vector_rows[:], identity_f32[:])
-            nc.vector.tensor_copy(columns[:], columns_ps[:, 0 : 4 * HEADS])
-            nc.vector.tensor_scalar_mul(q_scale[:], rel_col, 1.0 / math.sqrt(P))
-            nc.vector.tensor_mul(q_bias[:], b_head_col, q_scale[:])
+            nc.vector.tensor_scalar_mul(q_scale[:], rel_col[:], 1.0 / math.sqrt(P))
+            nc.vector.tensor_mul(q_bias[:], b_head_col[:], q_scale[:])
             for c in range(HEADS):
                 nc.gpsimd.tensor_scalar(b_out_wide[c][:], zeros[:], b_out_col[:, c : c + 1], 1.0, ALU.add, ALU.mult)
 
@@ -215,13 +212,14 @@ def tile_t2gformer_mae_b_kernel(
         y_first = results.tile([P, TOKENS], F32, name="y_sb")
         steps = list(product(range(GROUPS), range(HEADS)))
         fv_of_group = {g: [] for g in range(GROUPS)}
-        for j in range(GROUP // P):
-            fv_of_group[0].append(project_values(0, j))
         spread_vectors()
         q_sb, k_sb = project_q(0, 0), project_k(0, 0)
         make_mask(0)
         for n, (g, h) in enumerate(steps):
             score_0 = scores(q_sb, k_sb, 0)
+            if n == 0:
+                for j in range(GROUP // P):
+                    fv_of_group[0].append(project_values(0, j))
             if n + 1 < len(steps):
                 q_next = project_q(*steps[n + 1])
             e_0 = exponentials(score_0, h)

@@ -18,6 +18,7 @@ SLOTS = 4096
 GROUP = 512
 GROUPS = TOKENS // GROUP
 SAMPLES_PER_GROUP = GROUP // PLACES
+LAG = HEADS
 MASKED = -30000.0
 
 FLOPS = 4 * 2 * CHANNELS * CHANNELS * TOKENS + 2 * 2 * (TOKENS // PLACES) * HEADS * P * PLACES * PLACES
@@ -37,12 +38,13 @@ def tile_t2gformer_mae_b_kernel(
         tc.tile_pool(name="projected", bufs=3) as projected,
         tc.tile_pool(name="values", bufs=2 * GROUP // P) as values,
         tc.tile_pool(name="softmax", bufs=3) as softmax,
-        tc.tile_pool(name="weights", bufs=4) as weights,
+        tc.tile_pool(name="weights", bufs=2 * SAMPLES_PER_GROUP) as weights,
+        tc.tile_pool(name="flipped_weights", bufs=LAG + 1) as flipped_weights,
         tc.tile_pool(name="results", bufs=2) as results,
         tc.psum_pool(name="psum_proj", bufs=3) as psum_proj,
         tc.psum_pool(name="psum_score", bufs=2) as psum_score,
-        tc.psum_pool(name="psum_flip", bufs=2) as psum_flip,
-        tc.psum_pool(name="psum_att", bufs=1) as psum_att,
+        tc.psum_pool(name="psum_flip", bufs=1) as psum_flip,
+        tc.psum_pool(name="psum_att", bufs=2) as psum_att,
     ):
         identity = held.tile([P, P], BF16, name="identity")
         make_identity(nc, identity[:])
@@ -180,10 +182,11 @@ def tile_t2gformer_mae_b_kernel(
                 nc.vector.tensor_scalar_mul(p[:, c, :], e[:, c, :], one_over_sum[:, c : c + 1])
             return p
 
-        def flip(p):
-            p_flipped_ps = psum_flip.tile([P, HALVES, PLACES], BF16, name="flip_ps")
-            flip_256(p_flipped_ps, p)
-            p_flipped = weights.tile([P, HALVES, PLACES], BF16, name="p_flipped")
+        def flip(p_of_sample):
+            p_flipped_ps = psum_flip.tile([P, SAMPLES_PER_GROUP, HALVES, PLACES], BF16, name="flip_ps")
+            for s in range(SAMPLES_PER_GROUP):
+                flip_256(p_flipped_ps[:, s], p_of_sample[s])
+            p_flipped = flipped_weights.tile([P, SAMPLES_PER_GROUP, HALVES, PLACES], BF16, name="p_flipped")
             nc.vector.tensor_copy(p_flipped[:], p_flipped_ps[:])
             return p_flipped
 
@@ -195,7 +198,7 @@ def tile_t2gformer_mae_b_kernel(
                     nc.tensor.matmul(
                         att_ps[:, block(s, PLACES)],
                         fv_sb[HALVES * s + a][:, block(h)],
-                        flipped[s][:, a, :],
+                        flipped[:, s, a, :],
                         start=(a == 0),
                         stop=(a == HALVES - 1),
                     )
@@ -212,35 +215,34 @@ def tile_t2gformer_mae_b_kernel(
         y_first = results.tile([P, TOKENS], F32, name="y_sb")
         steps = list(product(range(GROUPS), range(HEADS)))
         fv_of_group = {g: [] for g in range(GROUPS)}
+        flipped_of_step = {}
         spread_vectors()
         q_sb, k_sb = project_q(0, 0), project_k(0, 0)
         make_mask(0)
         for n, (g, h) in enumerate(steps):
             score_0 = scores(q_sb, k_sb, 0)
-            if n == 0:
-                for j in range(GROUP // P):
-                    fv_of_group[0].append(project_values(0, j))
-            if n + 1 < len(steps):
-                q_next = project_q(*steps[n + 1])
-            e_0 = exponentials(score_0, h)
             score_1 = scores(q_sb, k_sb, 1)
+            e_0 = exponentials(score_0, h)
             if n + 1 < len(steps):
-                k_next = project_k(*steps[n + 1])
+                q_next, k_next = project_q(*steps[n + 1]), project_k(*steps[n + 1])
             e_1 = exponentials(score_1, h)
+            if n >= LAG:
+                weighted_sums(*steps[n - LAG], flipped_of_step[n - LAG])
+            p_0 = normalise(*e_0)
+            if n > 0:
+                flipped_of_step[n - 1] = flip(p_of_sample)
+            p_of_sample = [p_0, normalise(*e_1)]
+            fv_of_group[g].append(project_values(g, h))
             if g == 0 and h + 1 < HEADS:
                 make_mask(h + 1)
-            if n > 0:
-                flipped = [flip(p) for p in p_of_sample]
-            if g + 1 < GROUPS:
-                fv_of_group[g + 1].append(project_values(g + 1, h))
-            if n > 0:
-                weighted_sums(*steps[n - 1], flipped)
-            p_of_sample = [normalise(*e_0), normalise(*e_1)]
             q_sb, k_sb = q_next, k_next
-        for g in range(GROUPS - 1):
-            project_out(0, g, y_first)
-        weighted_sums(*steps[-1], [flip(p) for p in p_of_sample])
-        project_out(0, GROUPS - 1, y_first)
+        project_out(0, 0, y_first)
+        project_out(0, 1, y_first)
+        flipped_of_step[len(steps) - 1] = flip(p_of_sample)
+        for n in range(len(steps) - LAG, len(steps)):
+            weighted_sums(*steps[n], flipped_of_step[n])
+        project_out(0, 2, y_first)
+        project_out(0, 3, y_first)
 
         place(0, y_first)
         for c in range(1, HEADS):

@@ -64,19 +64,27 @@ def tile_t2gformer_mae_b_kernel(
             queue.dma_start(column[:], v.rearrange("(a p) o -> p (a o)", p=P))
             return column
 
-        w_head_sb = load_weights(nc.sync, w_head, "w_head_sb")
-        xh_sb = [load_tokens(nc.scalar, x_head, 0, "xh_sb")]
-        xt_sb = [load_tokens(nc.sync, x_tail, 0, "xt_sb")]
         rel_col = load_column(nc.scalar, rel, "rel_col")
         b_head_col = load_column(nc.scalar, b_head, "b_head_col")
-        w_v_sb = load_weights(nc.scalar, w_v, "w_v_sb")
+        b_v_col = load_column(nc.scalar, b_v, "b_v_col")
+        b_out_col = load_column(nc.scalar, b_out, "b_out_col")
+        w_head_sb = held.tile([P, HEADS, CHANNELS], BF16, name="w_head_sb")
+        xh_first = inputs.tile([P, HEADS, GROUP], BF16, name="xh_sb")
+        xt_first = inputs.tile([P, HEADS, GROUP], BF16, name="xt_sb")
+        for x_sb, x in ((xh_first, x_head), (xt_first, x_tail)):
+            for half in range(2):
+                blocks = block(half, HEADS // 2)
+                if x_sb is xh_first:
+                    nc.sync.dma_start(w_head_sb[:, blocks, :], w_head.rearrange("(a p) c -> p a c", p=P)[:, blocks, :])
+                nc.sync.dma_start(x_sb[:, blocks, :], x.rearrange("(a p) n -> p a n", p=P)[:, blocks, 0:GROUP])
+        xh_sb, xt_sb = [xh_first], [xt_first]
+        topo_sb = held.tile([P, HEADS, HALVES, PLACES], F32, name="topo_sb")
+        nc.sync.dma_start(topo_sb[:, 0], topo[0].rearrange("(a p) i -> p a i", p=P))
+        w_v_sb = load_weights(nc.sync, w_v, "w_v_sb")
+        for h in range(1, HEADS):
+            nc.sync.dma_start(topo_sb[:, h], topo[h].rearrange("(a p) i -> p a i", p=P))
         offsets = held.tile([P, TOKENS // 16], U16, name="offsets")
         nc.sync.dma_start(offsets[:], offs)
-        topo_sb = held.tile([P, HEADS, HALVES, PLACES], F32, name="topo_sb")
-        for h in range(HEADS):
-            nc.sync.dma_start(topo_sb[:, h], topo[h].rearrange("(a p) i -> p a i", p=P))
-        b_v_col = load_column(nc.sync, b_v, "b_v_col")
-        b_out_col = load_column(nc.sync, b_out, "b_out_col")
         for g in range(1, GROUPS):
             xt_sb.append(load_tokens(nc.sync, x_tail, g, "xt_sb"))
             xh_sb.append(load_tokens(nc.sync, x_head, g, "xh_sb"))

@@ -66,8 +66,6 @@ def tile_t2gformer_mae_b_kernel(
 
         rel_col = load_column(nc.scalar, rel, "rel_col")
         b_head_col = load_column(nc.scalar, b_head, "b_head_col")
-        b_v_col = load_column(nc.scalar, b_v, "b_v_col")
-        b_out_col = load_column(nc.scalar, b_out, "b_out_col")
         w_head_sb = held.tile([P, HEADS, CHANNELS], BF16, name="w_head_sb")
         xh_first = inputs.tile([P, HEADS, GROUP], BF16, name="xh_sb")
         xt_first = inputs.tile([P, HEADS, GROUP], BF16, name="xt_sb")
@@ -85,6 +83,8 @@ def tile_t2gformer_mae_b_kernel(
             nc.sync.dma_start(topo_sb[:, h], topo[h].rearrange("(a p) i -> p a i", p=P))
         offsets = held.tile([P, TOKENS // 16], U16, name="offsets")
         nc.sync.dma_start(offsets[:], offs)
+        b_v_col = load_column(nc.sync, b_v, "b_v_col")
+        b_out_col = load_column(nc.sync, b_out, "b_out_col")
         for g in range(1, GROUPS):
             xt_sb.append(load_tokens(nc.sync, x_tail, g, "xt_sb"))
             xh_sb.append(load_tokens(nc.sync, x_head, g, "xh_sb"))

@@ -169,11 +169,17 @@ def tile_t2gformer_mae_b_kernel(
                 )
             return score_ps
 
-        def exponentials(score_ps, h):
+        def add_mask(score_ps, h):
             score = softmax.tile([P, HALVES, PLACES], F32, name="score")
             nc.vector.tensor_tensor(score[:], score_ps[:], mask[:, h], ALU.add)
+            return score
+
+        def row_maxima(score):
             minus_max = softmax.tile([P, HALVES], F32, name="minus_max")
             nc.vector.reduce_max(minus_max[:], score[:], axis=mybir.AxisListType.X, negate=True)
+            return minus_max
+
+        def exponentials(score, minus_max):
             e = softmax.tile([P, HALVES, PLACES], F32, name="e")
             e_sum = softmax.tile([P, HALVES], F32, name="e_sum")
             for c in range(HALVES):
@@ -182,9 +188,12 @@ def tile_t2gformer_mae_b_kernel(
                 )
             return e, e_sum
 
-        def normalise(e, e_sum):
+        def invert(e_sum):
             one_over_sum = softmax.tile([P, HALVES], F32, name="one_over_sum")
             nc.vector.reciprocal(one_over_sum[:], e_sum[:])
+            return one_over_sum
+
+        def normalise(e, one_over_sum):
             p = weights.tile([P, HALVES, PLACES], BF16, name="p")
             for c in range(HALVES):
                 nc.vector.tensor_scalar_mul(p[:, c, :], e[:, c, :], one_over_sum[:, c : c + 1])
@@ -228,18 +237,20 @@ def tile_t2gformer_mae_b_kernel(
         q_sb, k_sb = project_q(0, 0), project_k(0, 0)
         make_mask(0)
         for n, (g, h) in enumerate(steps):
-            score_0 = scores(q_sb, k_sb, 0)
-            score_1 = scores(q_sb, k_sb, 1)
-            e_0 = exponentials(score_0, h)
+            score_ps = [scores(q_sb, k_sb, s) for s in range(SAMPLES_PER_GROUP)]
+            score = [add_mask(ps, h) for ps in score_ps]
+            minus_max = [row_maxima(masked) for masked in score]
+            e_0, e_sum_0 = exponentials(score[0], minus_max[0])
             if n + 1 < len(steps):
                 q_next, k_next = project_q(*steps[n + 1]), project_k(*steps[n + 1])
-            e_1 = exponentials(score_1, h)
+            e_1, e_sum_1 = exponentials(score[1], minus_max[1])
             if n >= LAG:
                 weighted_sums(*steps[n - LAG], flipped_of_step[n - LAG])
-            p_0 = normalise(*e_0)
+            one_over_sum_0 = invert(e_sum_0)
             if n > 0:
                 flipped_of_step[n - 1] = flip(p_of_sample)
-            p_of_sample = [p_0, normalise(*e_1)]
+            one_over_sum_1 = invert(e_sum_1)
+            p_of_sample = [normalise(e_0, one_over_sum_0), normalise(e_1, one_over_sum_1)]
             fv_of_group[g].append(project_values(g, h))
             if g == 0 and h + 1 < HEADS:
                 make_mask(h + 1)

@@ -113,15 +113,18 @@ def tile_t2gformer_mae_b_kernel(
 
         q_scale = held.tile([P, HEADS], F32, name="q_scale")
         q_bias = held.tile([P, HEADS], F32, name="q_bias")
-        zeros = held.tile([P, TOKENS], F32, name="zeros")
+        zeros = held.tile([P, GROUP], F32, name="zeros")
         nc.gpsimd.memset(zeros[:], 0.0)
         b_out_wide = [held.tile([P, TOKENS], F32, name=f"b_out_wide{c}") for c in range(HEADS)]
 
         def spread_vectors():
             nc.vector.tensor_scalar_mul(q_scale[:], rel_col[:], 1.0 / math.sqrt(P))
             nc.vector.tensor_mul(q_bias[:], b_head_col[:], q_scale[:])
-            for c in range(HEADS):
-                nc.gpsimd.tensor_scalar(b_out_wide[c][:], zeros[:], b_out_col[:, c : c + 1], 1.0, ALU.add, ALU.mult)
+
+        def spread_b_out(c, quarter):
+            nc.gpsimd.tensor_scalar(
+                b_out_wide[c][:, block(quarter, GROUP)], zeros[:], 1.0, b_out_col[:, c : c + 1], ALU.mult, ALU.add
+            )
 
         att_sb = held.tile([P, HEADS, TOKENS], BF16, name="att_sb")
 
@@ -196,7 +199,7 @@ def tile_t2gformer_mae_b_kernel(
         def normalise(e, one_over_sum):
             p = weights.tile([P, HALVES, PLACES], BF16, name="p")
             for c in range(HALVES):
-                nc.vector.tensor_scalar_mul(p[:, c, :], e[:, c, :], one_over_sum[:, c : c + 1])
+                nc.gpsimd.tensor_scalar(p[:, c, :], e[:, c, :], one_over_sum[:, c : c + 1], 0.0, ALU.mult, ALU.add)
             return p
 
         def flip(p_of_sample):
@@ -251,6 +254,7 @@ def tile_t2gformer_mae_b_kernel(
                 flipped_of_step[n - 1] = flip(p_of_sample)
             one_over_sum_1 = invert(e_sum_1)
             p_of_sample = [normalise(e_0, one_over_sum_0), normalise(e_1, one_over_sum_1)]
+            spread_b_out(g, h)
             fv_of_group[g].append(project_values(g, h))
             if g == 0 and h + 1 < HEADS:
                 make_mask(h + 1)

@@ -19,6 +19,7 @@ GROUP = 512
 GROUPS = TOKENS // GROUP
 SAMPLES_PER_GROUP = GROUP // PLACES
 LAG = HEADS
+FLIP_LAG = 2
 MASKED = -30000.0
 
 FLOPS = 4 * 2 * CHANNELS * CHANNELS * TOKENS + 2 * 2 * (TOKENS // PLACES) * HEADS * P * PLACES * PLACES
@@ -38,7 +39,7 @@ def tile_t2gformer_mae_b_kernel(
         tc.tile_pool(name="projected", bufs=3) as projected,
         tc.tile_pool(name="values", bufs=2 * GROUP // P) as values,
         tc.tile_pool(name="softmax", bufs=3) as softmax,
-        tc.tile_pool(name="weights", bufs=2 * SAMPLES_PER_GROUP) as weights,
+        tc.tile_pool(name="weights", bufs=(FLIP_LAG + 1) * SAMPLES_PER_GROUP) as weights,
         tc.tile_pool(name="flipped_weights", bufs=LAG + 1) as flipped_weights,
         tc.tile_pool(name="results", bufs=2) as results,
         tc.psum_pool(name="psum_proj", bufs=3) as psum_proj,
@@ -235,6 +236,7 @@ def tile_t2gformer_mae_b_kernel(
         y_first = results.tile([P, TOKENS], F32, name="y_sb")
         steps = list(product(range(GROUPS), range(HEADS)))
         fv_of_group = {g: [] for g in range(GROUPS)}
+        p_of_step = {}
         flipped_of_step = {}
         spread_vectors()
         q_sb, k_sb = project_q(0, 0), project_k(0, 0)
@@ -250,10 +252,10 @@ def tile_t2gformer_mae_b_kernel(
             if n >= LAG:
                 weighted_sums(*steps[n - LAG], flipped_of_step[n - LAG])
             one_over_sum_0 = invert(e_sum_0)
-            if n > 0:
-                flipped_of_step[n - 1] = flip(p_of_sample)
+            if n >= FLIP_LAG:
+                flipped_of_step[n - FLIP_LAG] = flip(p_of_step[n - FLIP_LAG])
             one_over_sum_1 = invert(e_sum_1)
-            p_of_sample = [normalise(e_0, one_over_sum_0), normalise(e_1, one_over_sum_1)]
+            p_of_step[n] = [normalise(e_0, one_over_sum_0), normalise(e_1, one_over_sum_1)]
             spread_b_out(g, h)
             fv_of_group[g].append(project_values(g, h))
             if g == 0 and h + 1 < HEADS:
@@ -261,7 +263,8 @@ def tile_t2gformer_mae_b_kernel(
             q_sb, k_sb = q_next, k_next
         project_out(0, 0, y_first)
         project_out(0, 1, y_first)
-        flipped_of_step[len(steps) - 1] = flip(p_of_sample)
+        for n in range(len(steps) - FLIP_LAG, len(steps)):
+            flipped_of_step[n] = flip(p_of_step[n])
         for n in range(len(steps) - LAG, len(steps)):
             weighted_sums(*steps[n], flipped_of_step[n])
         project_out(0, 2, y_first)

@@ -19,6 +19,7 @@ GROUP = 512
 GROUPS = TOKENS // GROUP
 SAMPLES_PER_GROUP = GROUP // PLACES
 LAG = HEADS
+AHEAD = 2
 FLIP_LAG = 2
 MASKED = -30000.0
 
@@ -70,12 +71,12 @@ def tile_t2gformer_mae_b_kernel(
         w_head_sb = held.tile([P, HEADS, CHANNELS], BF16, name="w_head_sb")
         xh_first = inputs.tile([P, HEADS, GROUP], BF16, name="xh_sb")
         xt_first = inputs.tile([P, HEADS, GROUP], BF16, name="xt_sb")
-        for x_sb, x in ((xh_first, x_head), (xt_first, x_tail)):
-            for half in range(2):
-                blocks = block(half, HEADS // 2)
-                if x_sb is xh_first:
-                    nc.sync.dma_start(w_head_sb[:, blocks, :], w_head.rearrange("(a p) c -> p a c", p=P)[:, blocks, :])
-                nc.sync.dma_start(x_sb[:, blocks, :], x.rearrange("(a p) n -> p a n", p=P)[:, blocks, 0:GROUP])
+        w_head_blocks = w_head.rearrange("(a p) c -> p a c", p=P)
+        nc.sync.dma_start(w_head_sb[:, :, 0:P], w_head_blocks[:, :, 0:P])
+        for blocks in (slice(0, 1), slice(1, 2), slice(2, HEADS)):
+            nc.sync.dma_start(xh_first[:, blocks, :], x_head.rearrange("(a p) n -> p a n", p=P)[:, blocks, 0:GROUP])
+        nc.sync.dma_start(xt_first[:], x_tail.rearrange("(a p) n -> p a n", p=P)[:, :, 0:GROUP])
+        nc.sync.dma_start(w_head_sb[:, :, P:], w_head_blocks[:, :, P:])
         xh_sb, xt_sb = [xh_first], [xt_first]
         topo_sb = held.tile([P, HEADS, HALVES, PLACES], F32, name="topo_sb")
         nc.sync.dma_start(topo_sb[:, 0], topo[0].rearrange("(a p) i -> p a i", p=P))
@@ -197,10 +198,10 @@ def tile_t2gformer_mae_b_kernel(
             nc.vector.reciprocal(one_over_sum[:], e_sum[:])
             return one_over_sum
 
-        def normalise(e, one_over_sum):
+        def normalise(engine, e, one_over_sum):
             p = weights.tile([P, HALVES, PLACES], BF16, name="p")
             for c in range(HALVES):
-                nc.gpsimd.tensor_scalar(p[:, c, :], e[:, c, :], one_over_sum[:, c : c + 1], 0.0, ALU.mult, ALU.add)
+                engine.tensor_scalar(p[:, c, :], e[:, c, :], one_over_sum[:, c : c + 1], 0.0, ALU.mult, ALU.add)
             return p
 
         def flip(p_of_sample):
@@ -239,15 +240,18 @@ def tile_t2gformer_mae_b_kernel(
         p_of_step = {}
         flipped_of_step = {}
         spread_vectors()
-        q_sb, k_sb = project_q(0, 0), project_k(0, 0)
+        q_of_step, k_of_step = {}, {}
+        for n in range(AHEAD):
+            q_of_step[n], k_of_step[n] = project_q(*steps[n]), project_k(*steps[n])
         make_mask(0)
         for n, (g, h) in enumerate(steps):
-            score_ps = [scores(q_sb, k_sb, s) for s in range(SAMPLES_PER_GROUP)]
+            score_ps = [scores(q_of_step[n], k_of_step[n], s) for s in range(SAMPLES_PER_GROUP)]
             score = [add_mask(ps, h) for ps in score_ps]
             minus_max = [row_maxima(masked) for masked in score]
             e_0, e_sum_0 = exponentials(score[0], minus_max[0])
-            if n + 1 < len(steps):
-                q_next, k_next = project_q(*steps[n + 1]), project_k(*steps[n + 1])
+            if n + AHEAD < len(steps):
+                q_of_step[n + AHEAD] = project_q(*steps[n + AHEAD])
+                k_of_step[n + AHEAD] = project_k(*steps[n + AHEAD])
             e_1, e_sum_1 = exponentials(score[1], minus_max[1])
             if n >= LAG:
                 weighted_sums(*steps[n - LAG], flipped_of_step[n - LAG])
@@ -255,12 +259,12 @@ def tile_t2gformer_mae_b_kernel(
             if n >= FLIP_LAG:
                 flipped_of_step[n - FLIP_LAG] = flip(p_of_step[n - FLIP_LAG])
             one_over_sum_1 = invert(e_sum_1)
-            p_of_step[n] = [normalise(e_0, one_over_sum_0), normalise(e_1, one_over_sum_1)]
+            engine = nc.gpsimd if n + 1 < len(steps) else nc.vector
+            p_of_step[n] = [normalise(engine, e_0, one_over_sum_0), normalise(engine, e_1, one_over_sum_1)]
             spread_b_out(g, h)
             fv_of_group[g].append(project_values(g, h))
             if g == 0 and h + 1 < HEADS:
                 make_mask(h + 1)
-            q_sb, k_sb = q_next, k_next
         project_out(0, 0, y_first)
         project_out(0, 1, y_first)
         for n in range(len(steps) - FLIP_LAG, len(steps)):

@@ -45,8 +45,8 @@ def tile_t2gformer_mae_b_kernel(
         tc.tile_pool(name="results", bufs=2) as results,
         tc.psum_pool(name="psum_proj", bufs=3) as psum_proj,
         tc.psum_pool(name="psum_score", bufs=2) as psum_score,
-        tc.psum_pool(name="psum_flip", bufs=1) as psum_flip,
-        tc.psum_pool(name="psum_att", bufs=2) as psum_att,
+        tc.psum_pool(name="psum_flip", bufs=2) as psum_flip,
+        tc.psum_pool(name="psum_att", bufs=1) as psum_att,
     ):
         identity = held.tile([P, P], BF16, name="identity")
         make_identity(nc, identity[:])
@@ -132,17 +132,18 @@ def tile_t2gformer_mae_b_kernel(
 
         def project(w_sb, c, x_sb):
             proj_ps = psum_proj.tile([P, GROUP], F32, name="proj_ps")
+            tokens = x_sb.shape[-1]
             for k in range(HEADS):
                 nc.tensor.matmul(
-                    proj_ps[:], w_sb[:, k, block(c)], x_sb[:, k, :], start=(k == 0), stop=(k == HEADS - 1)
+                    proj_ps[:, 0:tokens], w_sb[:, k, block(c)], x_sb[:, k, :], start=(k == 0), stop=(k == HEADS - 1)
                 )
-            return proj_ps
+            return proj_ps[:, 0:tokens]
 
         def project_q(g, h):
             q_sb = projected.tile([P, GROUP], BF16, name="q_sb")
             nc.scalar.activation(
                 q_sb[:],
-                project(w_head_sb, h, xh_sb[g])[:],
+                project(w_head_sb, h, xh_sb[g]),
                 ACT.Identity,
                 bias=q_bias[:, h : h + 1],
                 scale=q_scale[:, h : h + 1],
@@ -152,7 +153,7 @@ def tile_t2gformer_mae_b_kernel(
         def project_k(g, h):
             k_sb = projected.tile([P, GROUP], BF16, name="k_sb")
             nc.scalar.activation(
-                k_sb[:], project(w_head_sb, h, xt_sb[g])[:], ACT.Identity, bias=b_head_col[:, h : h + 1]
+                k_sb[:], project(w_head_sb, h, xt_sb[g]), ACT.Identity, bias=b_head_col[:, h : h + 1]
             )
             return k_sb
 
@@ -205,16 +206,15 @@ def tile_t2gformer_mae_b_kernel(
             return p
 
         def flip(p_of_sample):
-            p_flipped_ps = psum_flip.tile([P, SAMPLES_PER_GROUP, HALVES, PLACES], BF16, name="flip_ps")
-            for s in range(SAMPLES_PER_GROUP):
-                flip_256(p_flipped_ps[:, s], p_of_sample[s])
             p_flipped = flipped_weights.tile([P, SAMPLES_PER_GROUP, HALVES, PLACES], BF16, name="p_flipped")
-            nc.vector.tensor_copy(p_flipped[:], p_flipped_ps[:])
+            for s in range(SAMPLES_PER_GROUP):
+                p_flipped_ps = psum_flip.tile([P, HALVES, PLACES], BF16, name="flip_ps")
+                flip_256(p_flipped_ps, p_of_sample[s])
+                nc.vector.tensor_copy(p_flipped[:, s], p_flipped_ps[:])
             return p_flipped
 
-        def weighted_sums(g, h, flipped):
+        def weighted_sums(g, h, flipped, att_ps):
             fv_sb = fv_of_group[g]
-            att_ps = psum_att.tile([P, GROUP], F32, name="att_ps")
             for s in range(SAMPLES_PER_GROUP):
                 for a in range(HALVES):
                     nc.tensor.matmul(
@@ -226,9 +226,8 @@ def tile_t2gformer_mae_b_kernel(
                     )
             nc.scalar.activation(att_sb[:, h, block(g, GROUP)], att_ps[:], ACT.Identity, bias=b_v_col[:, h : h + 1])
 
-        def project_out(c, g, y_sb):
-            y_ps = project(w_out_sb, c, att_sb[:, :, block(g, GROUP)])
-            nc.scalar.copy(y_sb[:, block(g, GROUP)], y_ps[:])
+        def project_out(c, tokens, y_sb):
+            nc.scalar.copy(y_sb[:, tokens], project(w_out_sb, c, att_sb[:, :, tokens]))
 
         def place(c, y_sb):
             nc.vector.tensor_tensor(windows[c][:].indirect(offsets[:]), y_sb[:], b_out_wide[c][:], ALU.add)
@@ -254,7 +253,8 @@ def tile_t2gformer_mae_b_kernel(
                 k_of_step[n + AHEAD] = project_k(*steps[n + AHEAD])
             e_1, e_sum_1 = exponentials(score[1], minus_max[1])
             if n >= LAG:
-                weighted_sums(*steps[n - LAG], flipped_of_step[n - LAG])
+                att_ps = psum_att.tile([P, GROUP], F32, name="att_ps")
+                weighted_sums(*steps[n - LAG], flipped_of_step[n - LAG], att_ps)
             one_over_sum_0 = invert(e_sum_0)
             if n >= FLIP_LAG:
                 flipped_of_step[n - FLIP_LAG] = flip(p_of_step[n - FLIP_LAG])
@@ -265,18 +265,21 @@ def tile_t2gformer_mae_b_kernel(
             fv_of_group[g].append(project_values(g, h))
             if g == 0 and h + 1 < HEADS:
                 make_mask(h + 1)
-        project_out(0, 0, y_first)
-        project_out(0, 1, y_first)
+        project_out(0, block(0, GROUP), y_first)
+        project_out(0, block(1, GROUP), y_first)
         for n in range(len(steps) - FLIP_LAG, len(steps)):
             flipped_of_step[n] = flip(p_of_step[n])
         for n in range(len(steps) - LAG, len(steps)):
-            weighted_sums(*steps[n], flipped_of_step[n])
-        project_out(0, 2, y_first)
-        project_out(0, 3, y_first)
+            att_ps = psum_score.tile([P, GROUP], F32, name="last_att_ps", tag="score_ps")
+            weighted_sums(*steps[n], flipped_of_step[n], att_ps)
+        project_out(0, block(2, GROUP), y_first)
+        sample_6, sample_7 = block(6, PLACES), block(7, PLACES)
+        project_out(0, sample_6, y_first)
+        nc.vector.tensor_copy(y_first[:, sample_7], project(w_out_sb, 0, att_sb[:, :, sample_7]))
 
         place(0, y_first)
         for c in range(1, HEADS):
             y_sb = results.tile([P, TOKENS], F32, name="y_sb")
             for g in range(GROUPS):
-                project_out(c, g, y_sb)
+                project_out(c, block(g, GROUP), y_sb)
             place(c, y_sb)

import math
from itertools import product

import concourse.mybir as mybir
from concourse.masks import make_identity

BF16, F32, U16 = mybir.dt.bfloat16, mybir.dt.float32, mybir.dt.uint16
ALU = mybir.AluOpType
ACT = mybir.ActivationFunctionType

P = 128
CHANNELS = 512
HEADS = CHANNELS // P
TOKENS = 2048
PLACES = 256
HALVES = PLACES // P
SLOTS = 4096
GROUP = 512
GROUPS = TOKENS // GROUP
SAMPLES_PER_GROUP = GROUP // PLACES
LAG = HEADS
AHEAD = 2
FLIP_LAG = 2
MASKED = -30000.0

FLOPS = 4 * 2 * CHANNELS * CHANNELS * TOKENS + 2 * 2 * (TOKENS // PLACES) * HEADS * P * PLACES * PLACES


def block(i, size=P):
    return slice(i * size, (i + 1) * size)


def tile_t2gformer_mae_b_kernel(
    tc, base, x_head, x_tail, w_head, b_head, w_v, b_v, w_out, b_out, rel, topo, offs, out
):
    nc = tc.nc
    with (
        tc.tile_pool(name="held", bufs=1) as held,
        tc.tile_pool(name="inputs", bufs=GROUPS) as inputs,
        tc.tile_pool(name="projected", bufs=3) as projected,
        tc.tile_pool(name="values", bufs=2 * GROUP // P) as values,
        tc.tile_pool(name="softmax", bufs=3) as softmax,
        tc.tile_pool(name="weights", bufs=(FLIP_LAG + 1) * SAMPLES_PER_GROUP) as weights,
        tc.tile_pool(name="flipped_weights", bufs=LAG + 1) as flipped_weights,
        tc.tile_pool(name="results", bufs=2) as results,
        tc.psum_pool(name="psum_proj", bufs=3) as psum_proj,
        tc.psum_pool(name="psum_score", bufs=2) as psum_score,
        tc.psum_pool(name="psum_flip", bufs=2) as psum_flip,
        tc.psum_pool(name="psum_att", bufs=1) as psum_att,
    ):
        identity = held.tile([P, P], BF16, name="identity")
        make_identity(nc, identity[:])

        def load_weights(queue, w, name):
            w_sb = held.tile([P, HEADS, CHANNELS], BF16, name=name)
            queue.dma_start(w_sb[:], w.rearrange("(a p) c -> p a c", p=P))
            return w_sb

        def load_tokens(queue, x, g, name):
            x_sb = inputs.tile([P, HEADS, GROUP], BF16, name=name)
            queue.dma_start(x_sb[:], x.rearrange("(a p) n -> p a n", p=P)[:, :, block(g, GROUP)])
            return x_sb

        def load_column(queue, v, name):
            column = held.tile([P, HEADS], F32, name=name)
            queue.dma_start(column[:], v.rearrange("(a p) o -> p (a o)", p=P))
            return column

        rel_col = load_column(nc.scalar, rel, "rel_col")
        b_head_col = load_column(nc.scalar, b_head, "b_head_col")
        w_head_sb = held.tile([P, HEADS, CHANNELS], BF16, name="w_head_sb")
        xh_first = inputs.tile([P, HEADS, GROUP], BF16, name="xh_sb")
        xt_first = inputs.tile([P, HEADS, GROUP], BF16, name="xt_sb")
        w_head_blocks = w_head.rearrange("(a p) c -> p a c", p=P)
        nc.sync.dma_start(w_head_sb[:, :, 0:P], w_head_blocks[:, :, 0:P])
        for blocks in (slice(0, 1), slice(1, 2), slice(2, HEADS)):
            nc.sync.dma_start(xh_first[:, blocks, :], x_head.rearrange("(a p) n -> p a n", p=P)[:, blocks, 0:GROUP])
        nc.sync.dma_start(xt_first[:], x_tail.rearrange("(a p) n -> p a n", p=P)[:, :, 0:GROUP])
        nc.sync.dma_start(w_head_sb[:, :, P:], w_head_blocks[:, :, P:])
        xh_sb, xt_sb = [xh_first], [xt_first]
        topo_sb = held.tile([P, HEADS, HALVES, PLACES], F32, name="topo_sb")
        nc.sync.dma_start(topo_sb[:, 0], topo[0].rearrange("(a p) i -> p a i", p=P))
        w_v_sb = load_weights(nc.sync, w_v, "w_v_sb")
        for h in range(1, HEADS):
            nc.sync.dma_start(topo_sb[:, h], topo[h].rearrange("(a p) i -> p a i", p=P))
        offsets = held.tile([P, TOKENS // 16], U16, name="offsets")
        nc.sync.dma_start(offsets[:], offs)
        b_v_col = load_column(nc.sync, b_v, "b_v_col")
        b_out_col = load_column(nc.sync, b_out, "b_out_col")
        for g in range(1, GROUPS):
            xt_sb.append(load_tokens(nc.sync, x_tail, g, "xt_sb"))
            xh_sb.append(load_tokens(nc.sync, x_head, g, "xh_sb"))
        w_out_sb = load_weights(nc.sync, w_out, "w_out_sb")
        windows = [held.tile([P, SLOTS], F32, name=f"window{c}") for c in range(HEADS)]
        for c in range(HEADS):
            nc.sync.dma_start(windows[c][:], base[block(c), :])

        def flip_256(out_ps, in_sb):
            for x, y in product(range(HALVES), range(HALVES)):
                nc.tensor.transpose(out_ps[:, x, block(y)], in_sb[:, y, block(x)], identity[:])

        never = held.tile([P, HALVES, PLACES], BF16, name="never")
        nc.vector.memset(never[:], 0.0)
        for c in range(HALVES):
            nc.vector.tensor_scalar_mul(never[:, c, block(c)], identity[:], MASKED)
        nc.vector.memset(never[:, :, 0:1], MASKED)
        mask_ti = held.tile([P, HEADS, HALVES, PLACES], BF16, name="mask_ti")
        mask = held.tile([P, HEADS, HALVES, PLACES], BF16, name="mask")

        def make_mask(h):
            nc.vector.tensor_scalar(mask_ti[:, h], topo_sb[:, h], 1.0, -MASKED, ALU.subtract, ALU.mult)
            mask_ps = psum_flip.tile([P, HALVES, PLACES], BF16, name="flip_ps")
            flip_256(mask_ps, mask_ti[:, h])
            nc.vector.tensor_tensor(mask[:, h], mask_ps[:], never[:], ALU.add)

        q_scale = held.tile([P, HEADS], F32, name="q_scale")
        q_bias = held.tile([P, HEADS], F32, name="q_bias")
        zeros = held.tile([P, GROUP], F32, name="zeros")
        nc.gpsimd.memset(zeros[:], 0.0)
        b_out_wide = [held.tile([P, TOKENS], F32, name=f"b_out_wide{c}") for c in range(HEADS)]

        def spread_vectors():
            nc.vector.tensor_scalar_mul(q_scale[:], rel_col[:], 1.0 / math.sqrt(P))
            nc.vector.tensor_mul(q_bias[:], b_head_col[:], q_scale[:])

        def spread_b_out(c, quarter):
            nc.gpsimd.tensor_scalar(
                b_out_wide[c][:, block(quarter, GROUP)], zeros[:], 1.0, b_out_col[:, c : c + 1], ALU.mult, ALU.add
            )

        att_sb = held.tile([P, HEADS, TOKENS], BF16, name="att_sb")

        def project(w_sb, c, x_sb):
            proj_ps = psum_proj.tile([P, GROUP], F32, name="proj_ps")
            tokens = x_sb.shape[-1]
            for k in range(HEADS):
                nc.tensor.matmul(
                    proj_ps[:, 0:tokens], w_sb[:, k, block(c)], x_sb[:, k, :], start=(k == 0), stop=(k == HEADS - 1)
                )
            return proj_ps[:, 0:tokens]

        def project_q(g, h):
            q_sb = projected.tile([P, GROUP], BF16, name="q_sb")
            nc.scalar.activation(
                q_sb[:],
                project(w_head_sb, h, xh_sb[g]),
                ACT.Identity,
                bias=q_bias[:, h : h + 1],
                scale=q_scale[:, h : h + 1],
            )
            return q_sb

        def project_k(g, h):
            k_sb = projected.tile([P, GROUP], BF16, name="k_sb")
            nc.scalar.activation(
                k_sb[:], project(w_head_sb, h, xt_sb[g]), ACT.Identity, bias=b_head_col[:, h : h + 1]
            )
            return k_sb

        def project_values(g, j):
            fv_ps = psum_proj.tile([P, CHANNELS], F32, name="proj_ps")
            for k in range(HEADS):
                nc.tensor.matmul(
                    fv_ps[:], xt_sb[g][:, k, block(j)], w_v_sb[:, k, :], start=(k == 0), stop=(k == HEADS - 1)
                )
            fv_sb = values.tile([P, CHANNELS], BF16, name="fv_sb")
            nc.scalar.copy(fv_sb[:], fv_ps[:])
            return fv_sb

        def scores(q_sb, k_sb, s):
            score_ps = psum_score.tile([P, HALVES, PLACES], F32, name="score_ps")
            for c in range(HALVES):
                nc.tensor.matmul(
                    score_ps[:, c, :], q_sb[:, block(HALVES * s + c)], k_sb[:, block(s, PLACES)], start=True, stop=True
                )
            return score_ps

        def add_mask(score_ps, h):
            score = softmax.tile([P, HALVES, PLACES], F32, name="score")
            nc.vector.tensor_tensor(score[:], score_ps[:], mask[:, h], ALU.add)
            return score

        def row_maxima(score):
            minus_max = softmax.tile([P, HALVES], F32, name="minus_max")
            nc.vector.reduce_max(minus_max[:], score[:], axis=mybir.AxisListType.X, negate=True)
            return minus_max

        def exponentials(score, minus_max):
            e = softmax.tile([P, HALVES, PLACES], F32, name="e")
            e_sum = softmax.tile([P, HALVES], F32, name="e_sum")
            for c in range(HALVES):
                nc.scalar.activation(
                    e[:, c, :], score[:, c, :], ACT.Exp, bias=minus_max[:, c : c + 1], accum_out=e_sum[:, c : c + 1]
                )
            return e, e_sum

        def invert(e_sum):
            one_over_sum = softmax.tile([P, HALVES], F32, name="one_over_sum")
            nc.vector.reciprocal(one_over_sum[:], e_sum[:])
            return one_over_sum

        def normalise(engine, e, one_over_sum):
            p = weights.tile([P, HALVES, PLACES], BF16, name="p")
            for c in range(HALVES):
                engine.tensor_scalar(p[:, c, :], e[:, c, :], one_over_sum[:, c : c + 1], 0.0, ALU.mult, ALU.add)
            return p

        def flip(p_of_sample):
            p_flipped = flipped_weights.tile([P, SAMPLES_PER_GROUP, HALVES, PLACES], BF16, name="p_flipped")
            for s in range(SAMPLES_PER_GROUP):
                p_flipped_ps = psum_flip.tile([P, HALVES, PLACES], BF16, name="flip_ps")
                flip_256(p_flipped_ps, p_of_sample[s])
                nc.vector.tensor_copy(p_flipped[:, s], p_flipped_ps[:])
            return p_flipped

        def weighted_sums(g, h, flipped, att_ps):
            fv_sb = fv_of_group[g]
            for s in range(SAMPLES_PER_GROUP):
                for a in range(HALVES):
                    nc.tensor.matmul(
                        att_ps[:, block(s, PLACES)],
                        fv_sb[HALVES * s + a][:, block(h)],
                        flipped[:, s, a, :],
                        start=(a == 0),
                        stop=(a == HALVES - 1),
                    )
            nc.scalar.activation(att_sb[:, h, block(g, GROUP)], att_ps[:], ACT.Identity, bias=b_v_col[:, h : h + 1])

        def project_out(c, tokens, y_sb):
            nc.scalar.copy(y_sb[:, tokens], project(w_out_sb, c, att_sb[:, :, tokens]))

        def place(c, y_sb):
            nc.vector.tensor_tensor(windows[c][:].indirect(offsets[:]), y_sb[:], b_out_wide[c][:], ALU.add)
            nc.sync.dma_start(out[block(c), :], windows[c][:])

        y_first = results.tile([P, TOKENS], F32, name="y_sb")
        steps = list(product(range(GROUPS), range(HEADS)))
        fv_of_group = {g: [] for g in range(GROUPS)}
        p_of_step = {}
        flipped_of_step = {}
        spread_vectors()
        q_of_step, k_of_step = {}, {}
        for n in range(AHEAD):
            q_of_step[n], k_of_step[n] = project_q(*steps[n]), project_k(*steps[n])
        make_mask(0)
        for n, (g, h) in enumerate(steps):
            score_ps = [scores(q_of_step[n], k_of_step[n], s) for s in range(SAMPLES_PER_GROUP)]
            score = [add_mask(ps, h) for ps in score_ps]
            minus_max = [row_maxima(masked) for masked in score]
            e_0, e_sum_0 = exponentials(score[0], minus_max[0])
            if n + AHEAD < len(steps):
                q_of_step[n + AHEAD] = project_q(*steps[n + AHEAD])
                k_of_step[n + AHEAD] = project_k(*steps[n + AHEAD])
            e_1, e_sum_1 = exponentials(score[1], minus_max[1])
            if n >= LAG:
                att_ps = psum_att.tile([P, GROUP], F32, name="att_ps")
                weighted_sums(*steps[n - LAG], flipped_of_step[n - LAG], att_ps)
            one_over_sum_0 = invert(e_sum_0)
            if n >= FLIP_LAG:
                flipped_of_step[n - FLIP_LAG] = flip(p_of_step[n - FLIP_LAG])
            one_over_sum_1 = invert(e_sum_1)
            engine = nc.gpsimd if n + 1 < len(steps) else nc.vector
            p_of_step[n] = [normalise(engine, e_0, one_over_sum_0), normalise(engine, e_1, one_over_sum_1)]
            spread_b_out(g, h)
            fv_of_group[g].append(project_values(g, h))
            if g == 0 and h + 1 < HEADS:
                make_mask(h + 1)
        project_out(0, block(0, GROUP), y_first)
        project_out(0, block(1, GROUP), y_first)
        for n in range(len(steps) - FLIP_LAG, len(steps)):
            flipped_of_step[n] = flip(p_of_step[n])
        for n in range(len(steps) - LAG, len(steps)):
            att_ps = psum_score.tile([P, GROUP], F32, name="last_att_ps", tag="score_ps")
            weighted_sums(*steps[n], flipped_of_step[n], att_ps)
        project_out(0, block(2, GROUP), y_first)
        sample_6, sample_7 = block(6, PLACES), block(7, PLACES)
        project_out(0, sample_6, y_first)
        nc.vector.tensor_copy(y_first[:, sample_7], project(w_out_sb, 0, att_sb[:, :, sample_7]))

        place(0, y_first)
        for c in range(1, HEADS):
            y_sb = results.tile([P, TOKENS], F32, name="y_sb")
            for g in range(GROUPS):
                project_out(c, block(g, GROUP), y_sb)
            place(c, y_sb)
